import numpy as np
import ml_dtypes


def mxq(x, axis, fmt="e4m3"):
    dtype, down = {"e4m3": (ml_dtypes.float8_e4m3fn, 7), "e5m2": (ml_dtypes.float8_e5m2, 14)}[fmt]
    v = np.moveaxis(np.asarray(x, np.float32).astype(ml_dtypes.bfloat16).astype(np.float64), axis, -1)
    blocks = v.reshape(v.shape[:-1] + (-1, 32))
    amax = np.abs(blocks).max(-1, keepdims=True)
    byte = np.maximum(np.where(amax > 0, np.frexp(amax)[1] - 1 + 127, 0) - down, 1)
    scale = np.exp2(byte - 127.0)
    codes = (blocks / scale).astype(np.float32).astype(dtype).astype(np.float64)
    return np.moveaxis((codes * scale).reshape(v.shape), -1, axis)


WIDE = False


def mx_kscale(k):
    if not WIDE:
        return np.ones(k)
    levels = np.array([10, -10, 5, -5, 0])
    if k % 512:
        return np.exp2(np.random.permutation(np.resize(levels, k // 32))).repeat(32)
    a = np.empty((k // 512, 16))
    for p in range(k // 512):
        a[p, :8] = np.random.permutation(np.resize(levels, 8))
        for g in range(8):
            far = levels[np.abs(levels - a[p, g]) >= 10]
            a[p, g + 8] = far[np.random.randint(len(far))]
    return np.exp2(a.ravel()).repeat(32)


BF16 = ml_dtypes.bfloat16


def bf(x):
    return np.asarray(x, np.float32).astype(BF16)


def f64(x):
    return np.asarray(x).astype(np.float64)


B, S, M, H, HKV, DH, R_T, R_H, R_W = 2, 2048, 1024, 2, 1, 128, 16, 24, 24
SECT = (2 * R_T, 2 * R_H, 2 * R_W)
NC = len(SECT)


def rotate_half(x):
    h = x.shape[-1] // 2
    return np.concatenate((-x[..., h:], x[..., :h]), axis=-1)


def mrope_combine(t):
    parts, off = [], 0
    for i, sz in enumerate(SECT):
        parts.append(t[i % NC, :, :, off:off + sz])
        off += sz
    return np.concatenate(parts, axis=-1)


def setup_inputs():
    s = mx_kscale(M)
    sd = 1.0 / np.sqrt(M)
    return {"hidden_states": bf(np.random.standard_normal((B, S, M)) * s),
            "cos": bf(np.random.standard_normal((NC, B, S, DH))),
            "sin": bf(np.random.standard_normal((NC, B, S, DH))),
            "Wq": bf(np.random.standard_normal((M, H, DH)) * sd / s[:, None, None]),
            "bq": bf(np.random.standard_normal((H, DH)) * 0.3),
            "Wk": bf(np.random.standard_normal((M, HKV, DH)) * sd / s[:, None, None]),
            "bk": bf(np.random.standard_normal((HKV, DH)) * 0.3),
            "Wv": bf(np.random.standard_normal((M, HKV, DH)) * sd / s[:, None, None]),
            "bv": bf(np.random.standard_normal((HKV, DH)) * 0.3)}


def reference(hidden_states, cos, sin, Wq, bq, Wk, bk, Wv, bv):
    xq = mxq(f64(hidden_states), 2, "e4m3")
    q = (xq @ mxq(f64(Wq).reshape(M, H * DH), 0, "e4m3")).reshape(B, S, H, DH) + f64(bq)
    k = (xq @ mxq(f64(Wk).reshape(M, HKV * DH), 0, "e4m3")).reshape(B, S, HKV, DH) + f64(bk)
    v = (xq @ mxq(f64(Wv).reshape(M, HKV * DH), 0, "e4m3")).reshape(B, S, HKV, DH) + f64(bv)
    cos_c = mrope_combine(f64(cos))[:, :, None, :]
    sin_c = mrope_combine(f64(sin))[:, :, None, :]
    q_rot = q * cos_c + rotate_half(q) * sin_c
    k_rot = k * cos_c + rotate_half(k) * sin_c
    return q_rot, k_rot, v

@@ -1,0 +1,349 @@
+from contextlib import ExitStack
+
+import concourse.mybir as mybir
+from concourse.masks import make_identity
+
+F32 = mybir.dt.float32
+BF16 = mybir.dt.bfloat16
+U32 = mybir.dt.uint32
+U8 = mybir.dt.uint8
+FP8X4 = mybir.dt.float8_e4m3fn_x4
+ALU = mybir.AluOpType
+ACT = mybir.ActivationFunctionType
+
+P = 128
+NB = 2
+TS = 16
+M = 1024
+NROUND = 16
+NGROUP = 8
+XBUFS = 6
+OBUFS = 3
+
+FLOPS = 2 * 4096 * 1024 * 512
+BYTES = 4096 * 1024 * 2 + 1024 * 512 * 2 + 2 * 4096 * 128 * 2 + 512 * 2 + 4096 * 512 * 4
+
+TABLE_BATCHES = ((0, 0, 2), (0, 2, 2), (0, 4, 4), (0, 8, 4), (0, 12, 4), (1, 0, 4), (1, 4, 4), (1, 8, 4), (1, 12, 4))
+TABLE_LOADS = ((0, 0, 2), (0, 2, 2), (0, 4, 4), (0, 8, 4), (0, 12, 4), (1, 0, 8), (1, 8, 8))
+
+
+def tile_qwen2vlattention_pa_t_kernel(
+    tc, hidden_states, cos, sin, Wq, bq, Wk, bk, Wv, bv, out_0, out_1, out_2
+):
+    nc = tc.nc
+    with ExitStack() as ctx:
+        ctx.enter_context(tc.manual_schedule())
+        const = ctx.enter_context(tc.tile_pool(name="const", bufs=1))
+        xpool = ctx.enter_context(tc.tile_pool(name="xpool", bufs=XBUFS))
+        xgp = ctx.enter_context(tc.tile_pool(name="xgp", bufs=3))
+        xcp = ctx.enter_context(tc.tile_pool(name="xcp", bufs=4))
+        ytp = ctx.enter_context(tc.tile_pool(name="ytp", bufs=3))
+        ttp = ctx.enter_context(tc.tile_pool(name="ttp", bufs=2))
+        outp = ctx.enter_context(tc.tile_pool(name="outp", bufs=OBUFS))
+        psx = ctx.enter_context(tc.psum_pool(name="psx", bufs=2))
+        psm = ctx.enter_context(tc.psum_pool(name="psm", bufs=1))
+        psy = ctx.enter_context(tc.psum_pool(name="psy", bufs=4))
+
+        x_view = hidden_states.rearrange("b (p t) m -> b p t m", t=TS)
+        cos_view = cos.rearrange("c b (p t) d -> b p c t d", t=TS)
+        sin_view = sin.rearrange("c b (p t) d -> b p c t d", t=TS)
+        q_view = out_0.rearrange("b (p t) h d -> b p t (h d)", t=TS)
+        k_view = out_1.rearrange("b (p t) h d -> b p t (h d)", t=TS)
+        v_view = out_2.rearrange("b (p t) h d -> b p t (h d)", t=TS)
+
+        ident = const.tile([P, P], F32)
+        make_identity(nc, ident[:])
+
+        brow_bf = const.tile([P, P], BF16)
+        nc.vector.memset(brow_bf[:], 0.0)
+        warm = const.tile([P, 2], F32)
+        nc.vector.memset(warm[:], 0.0)
+        nc.scalar.dma_start(out=brow_bf[0:2, :], in_=bq)
+        nc.scalar.dma_start(out=brow_bf[2:3, :], in_=bk)
+        bvb = const.tile([P, P], BF16)
+        nc.scalar.dma_start(out=bvb[:], in_=bv.rearrange("o d -> (o d)").partition_broadcast(P))
+        nc.scalar.activation(out=warm[:, 1:2], in_=warm[:, 0:1], func=ACT.Identity, bias=0.0, scale=1.0)
+
+        xin = {}
+        raws = {}
+
+        def load_x(grp, parts):
+            xt_in = xpool.tile([P, 4, M], BF16, name="xin")
+            xin[grp] = xt_in
+            b, t0 = grp // 4, 4 * (grp % 4)
+            step = 4 // parts
+            return [
+                (xt_in[:, i * step : (i + 1) * step, :], x_view[b, :, t0 + i * step : t0 + (i + 1) * step, :])
+                for i in range(parts)
+            ]
+
+        def load_table(k):
+            b, t0, tn = TABLE_LOADS[k]
+            rawc = const.tile([P, 3, tn, P], BF16, name="rawc%d" % k)
+            nc.sync.dma_start(out=rawc[:], in_=cos_view[b, :, :, t0 : t0 + tn, :])
+            rawsn = const.tile([P, 3, tn, P], BF16, name="rawsn%d" % k)
+            nc.sync.dma_start(out=rawsn[:], in_=sin_view[b, :, :, t0 : t0 + tn, :])
+            for i in range(tn):
+                raws[(b, t0 + i)] = (rawc, rawsn, i)
+
+        def start(pair):
+            nc.sync.dma_start(out=pair[0], in_=pair[1])
+
+        halves = [load_x(grp, 2) for grp in range(3)]
+        start(halves[0][0])
+        wraw = ttp.tile([P, 4096], BF16, name="tt", align_bytes=64)
+        def load_w(w, c0, c1):
+            raw = wraw[:, c0:c1].rearrange("p (g c) -> p g c", g=2)
+            nc.sync.dma_start(out=raw, in_=w.rearrange("(g p f) h d -> p g (f h d)", g=2, f=4))
+            return wraw[:, c0:c1].rearrange("p (a c) -> p a c", a=4)
+
+        wraw_q = load_w(Wq, 0, 2048)
+        wraw_k = load_w(Wk, 2048, 3072)
+        wraw_v = load_w(Wv, 3072, 4096)
+        start(halves[0][1])
+        load_table(0)
+        start(halves[1][0])
+        load_table(1)
+        start(halves[1][1])
+        load_table(2)
+        start(halves[2][0])
+        start(halves[2][1])
+        for grp in (3, 4, 5):
+            load_table(grp)
+            start(load_x(grp, 1)[0])
+
+        wg = ttp.tile([P, 4, 2, P, 4], BF16, name="tt", align_bytes=64)
+        wc = const.tile([P, 4, 2, P], U32, align_bytes=64)
+        ws = const.tile([P, 4, 2, P], U8, align_bytes=64)
+
+        def w_source(h):
+            if h < 2:
+                v5 = wraw_q.rearrange("p (g u) (e c) -> p g u e c", g=2, e=2)
+                return v5[:, :, :, :, h * P : (h + 1) * P]
+            raw = wraw_k if h == 2 else wraw_v
+            return raw.rearrange("p (g u) (e c) -> p g u e c", g=2, e=2)
+
+        def w_regroup(h, engine):
+            src5 = w_source(h)
+            for g in range(2):
+                dst = wg[:, h, g].rearrange("p c (u e) -> p c u e", u=2)
+                src = src5[:, g].rearrange("p u e c -> p c u e")
+                if engine == "scalar":
+                    nc.scalar.copy(out=dst, in_=src)
+                elif engine == "gpsimd":
+                    nc.gpsimd.tensor_scalar(out=dst, in0=src, scalar1=1.0, scalar2=0.0, op0=ALU.mult, op1=ALU.add)
+                else:
+                    nc.vector.tensor_copy(out=dst, in_=src)
+
+        def w_quantise(h):
+            nc.vector.quantize_mx(
+                out=wc[:, h].rearrange("p g c -> p (g c)").bitcast(FP8X4),
+                scales=ws[:, h].rearrange("p g c -> p (g c)"),
+                in_=wg[:, h].rearrange("p g c t -> p (g c t)"),
+            )
+
+        cs_of = {}
+
+        def combine(k, on_vector):
+            b, t0, tn = TABLE_BATCHES[k]
+            rawc, rawsn, r0 = raws[(b, t0)]
+            cst = const.tile([P, tn, 2, P], BF16, name="cs%d" % k)
+            for i in range(tn):
+                cs_of[(b, t0 + i)] = (cst, i)
+            moves = [(0, raw_lo, raw_hi, rawc, comp, raw_lo) for raw_lo, raw_hi, comp in ((0, 32, 0), (32, 80, 1), (80, 128, 2))]
+            moves += [(1, lo, hi, rawsn, comp, s0) for lo, hi, comp, s0 in ((0, 16, 1, 64), (16, 64, 2, 80), (64, 96, 0, 0), (96, 128, 1, 32))]
+            for row, lo, hi, raw, comp, s0 in moves:
+                if on_vector:
+                    nc.vector.tensor_copy(out=cst[:, :, row, lo:hi], in_=raw[:, comp, r0 : r0 + tn, s0 : s0 + hi - lo])
+                else:
+                    nc.scalar.copy(out=cst[:, :, row, lo:hi], in_=raw[:, comp, r0 : r0 + tn, s0 : s0 + hi - lo])
+
+        xg_of, xc_of, yt_of, yb_of, tt_of, o_of = {}, {}, {}, {}, {}, {}
+        bias_col = const.tile([P, 4], F32)
+
+        def stage_a(r):
+            xt_in = xin[r // 2]
+            xg = xgp.tile([P, 1024], F32, align_bytes=64)
+            xg_of[r] = xg
+            for j in range(2):
+                words = xt_in[:, 2 * (r % 2) + j, :].bitcast(F32)
+                xt = psx.tile([P, 512], F32)
+                for i in range(4):
+                    g, u = i // 2, i % 2
+                    nc.tensor.transpose(xt[:, i * P : (i + 1) * P], words[:, 256 * g + u : 256 * (g + 1) : 2], ident[:])
+                nc.scalar.copy(
+                    out=xg[:].rearrange("p (g r u) -> p g r u", g=2, u=2)[:, :, j * P : (j + 1) * P, :],
+                    in_=xt[:].rearrange("p (g u r) -> p g r u", g=2, u=2),
+                )
+
+        def stage_q(r):
+            xc = xcp.tile([P, 512], U32, align_bytes=64)
+            xs = xcp.tile([P, 512], U8, align_bytes=64)
+            xc_of[r] = (xc, xs)
+            nc.vector.quantize_mx(out=xc[:].bitcast(FP8X4), scales=xs[:], in_=xg_of[r][:].bitcast(BF16))
+
+        def stage_b(r):
+            xc, xs = xc_of[r]
+            m0 = psm.tile([P, 2, 256], F32)
+            m1 = psm.tile([P, 256], F32)
+            yt = ytp.tile([P, 3, 256], F32)
+            yt_of[r] = yt
+            for h in range(3):
+                acc = m0[:, h, :] if h < 2 else m1[:]
+                for g in range(2):
+                    nc.tensor.matmul_mx(
+                        out=acc,
+                        lhsT=wc[:, h, g, :].bitcast(FP8X4),
+                        lhsT_scale=ws[:, h, g, :],
+                        rhs=xc[:, g * 256 : (g + 1) * 256].bitcast(FP8X4),
+                        rhs_scale=xs[:, g * 256 : (g + 1) * 256],
+                        start=(g == 0),
+                        stop=(g == 1),
+                    )
+            for h in range(3):
+                acc = m0[:, h, :] if h < 2 else m1[:]
+                nc.scalar.activation(
+                    out=yt[:, h, :], in_=acc, func=ACT.Identity, bias=bias_col[:, h : h + 1], scale=1.0
+                )
+
+        def stage_bv(r):
+            xc, xs = xc_of[r]
+            ybs = []
+            for j in range(2):
+                yb = psy.tile([P, 512], F32)
+                ybs.append(yb)
+                for g in range(2):
+                    c0 = g * 256 + j * P
+                    nc.tensor.matmul_mx(
+                        out=yb[:, 384:512],
+                        lhsT=xc[:, c0 : c0 + P].bitcast(FP8X4),
+                        lhsT_scale=xs[:, c0 : c0 + P],
+                        rhs=wc[:, 3, g, :].bitcast(FP8X4),
+                        rhs_scale=ws[:, 3, g, :],
+                        start=(g == 0),
+                        stop=(g == 1),
+                    )
+            yb_of[r] = ybs
+
+        def stage_dtr(r):
+            yt = yt_of[r]
+            for j in range(2):
+                for h in range(3):
+                    nc.tensor.transpose(
+                        yb_of[r][j][:, h * P : (h + 1) * P], yt[:, h, j * P : (j + 1) * P], ident[:]
+                    )
+
+        def stage_e(r):
+            grp = r // 2
+            if r % 4 == 0:
+                ov = outp.tile([P, 8, P], F32)
+                oq = outp.tile([P, 8, 256], F32)
+                ok = outp.tile([P, 8, P], F32)
+                o_of[grp // 2] = (ov, oq, ok)
+            if r % 2 == 0:
+                tt = ttp.tile([P, 4, 2, 3, P], F32, align_bytes=64)
+                tt_of[grp] = tt
+            tt = tt_of[grp]
+            ov = o_of[grp // 2][0]
+            b = grp // 4
+            for j in range(2):
+                t4 = 2 * (r % 2) + j
+                cst, ci = cs_of[(b, 4 * (grp % 4) + t4)]
+                yb = yb_of[r][j]
+                nc.vector.tensor_tensor(out=ov[:, 4 * (grp % 2) + t4, :], in0=yb[:, 384:512], in1=bvb[:], op=ALU.add)
+                nc.vector.tensor_tensor(
+                    out=tt[:, t4],
+                    in0=yb[:, 0:384].rearrange("p (h d) -> p h d", h=3).unsqueeze(1).to_broadcast([P, 2, 3, P]),
+                    in1=cst[:, ci].unsqueeze(2).to_broadcast([P, 2, 3, P]),
+                    op=ALU.mult,
+                )
+
+        def add_q(grp, ta, tb, engine):
+            tt = tt_of[grp]
+            so = 4 * (grp % 2)
+            oq4 = o_of[grp // 2][1][:, so : so + 4, :].rearrange("p t (h d) -> p t h d", h=2)
+            engine.tensor_tensor(
+                out=oq4[:, ta:tb, :, 0:64], in0=tt[:, ta:tb, 0, 0:2, 0:64], in1=tt[:, ta:tb, 1, 0:2, 64:128],
+                op=ALU.subtract,
+            )
+            engine.tensor_tensor(
+                out=oq4[:, ta:tb, :, 64:128], in0=tt[:, ta:tb, 0, 0:2, 64:128], in1=tt[:, ta:tb, 1, 0:2, 0:64],
+                op=ALU.add,
+            )
+
+        def add_k(grp, ta, tb):
+            tt = tt_of[grp]
+            so = 4 * (grp % 2)
+            ok = o_of[grp // 2][2][:, so : so + 4, :]
+            nc.vector.tensor_tensor(
+                out=ok[:, ta:tb, 0:64], in0=tt[:, ta:tb, 0, 2, 0:64], in1=tt[:, ta:tb, 1, 2, 64:128], op=ALU.subtract
+            )
+            nc.vector.tensor_tensor(
+                out=ok[:, ta:tb, 64:128], in0=tt[:, ta:tb, 0, 2, 64:128], in1=tt[:, ta:tb, 1, 2, 0:64], op=ALU.add
+            )
+
+        def stores(pair, ta, tb):
+            b, t0 = pair // 2, 8 * (pair % 2)
+            ov, oq, ok = o_of[pair]
+            nc.sync.dma_start(out=v_view[b, :, t0 + ta : t0 + tb, :], in_=ov[:, ta:tb, :])
+            nc.sync.dma_start(out=q_view[b, :, t0 + ta : t0 + tb, :], in_=oq[:, ta:tb, :])
+            nc.sync.dma_start(out=k_view[b, :, t0 + ta : t0 + tb, :], in_=ok[:, ta:tb, :])
+
+        first_round = [(8 * b + t0 // 2) for b, t0, tn in TABLE_BATCHES]
+        n_batches = len(TABLE_BATCHES)
+
+        def combines(s, on_vector):
+            for k in range(n_batches):
+                if (k < 2) != on_vector:
+                    continue
+                if s == first_round[k] + (2 if k < 2 else 1):
+                    combine(k, on_vector)
+
+        for s in range(NROUND + 2):
+            pending = []
+            if 2 <= s <= 2:
+                stage_dtr(s - 2)
+            if s < NROUND:
+                stage_a(s)
+            if s > 2:
+                stage_dtr(s - 2)
+            if s == 0:
+                brow_f = const.tile([P, P], F32)
+                nc.vector.tensor_copy(out=brow_f[:], in_=brow_bf[:])
+                bt = psm.tile([P, 256], F32, name="m1")
+                nc.tensor.transpose(bt[:, 0:P], brow_f[:], ident[:])
+                nc.vector.tensor_copy(out=bias_col[:], in_=bt[:, 0:4])
+                w_regroup(0, "vector")
+                w_regroup(1, "scalar")
+                stage_q(0)
+                w_regroup(2, "vector")
+                w_regroup(3, "scalar")
+                for h in range(4):
+                    w_quantise(h)
+            combines(s, True)
+            if s >= 2:
+                r = s - 2
+                stage_e(r)
+                grp = r // 2
+                ta = 2 * (r % 2)
+                add_q(grp, ta, ta + 2, nc.vector if r == NROUND - 1 else nc.gpsimd)
+                if grp == NGROUP - 1:
+                    pending.append((grp // 2, 4 + ta, 4 + ta + 2))
+                elif r % 2 == 1 and grp == NGROUP - 2:
+                    pending.append((grp // 2, 0, 4))
+                elif r % 4 == 3:
+                    pending.append((grp // 2, 0, 8))
+            if 0 < s < NROUND:
+                stage_q(s)
+            if s >= 2:
+                add_k((s - 2) // 2, 2 * (s % 2), 2 * (s % 2) + 2)
+            if 1 <= s <= NROUND:
+                stage_b(s - 1)
+                stage_bv(s - 1)
+            combines(s, False)
+            if s == 3:
+                load_table(6)
+            if s % 2 == 1 and s // 2 + XBUFS < NGROUP:
+                start(load_x(s // 2 + XBUFS, 1)[0])
+            for pair, ta, tb in pending:
+                stores(pair, ta, tb)

@@ -60,8 +60,8 @@ def tile_qwen2vlattention_pa_t_kernel(
         nc.vector.memset(warm[:], 0.0)
         nc.scalar.dma_start(out=brow_bf[0:2, :], in_=bq)
         nc.scalar.dma_start(out=brow_bf[2:3, :], in_=bk)
-        bvb = const.tile([P, P], BF16)
-        nc.scalar.dma_start(out=bvb[:], in_=bv.rearrange("o d -> (o d)").partition_broadcast(P))
+        nc.scalar.dma_start(out=brow_bf[3:4, :], in_=bv)
+        bvb = const.tile([P, P], F32)
         nc.scalar.activation(out=warm[:, 1:2], in_=warm[:, 0:1], func=ACT.Identity, bias=0.0, scale=1.0)
 
         xin = {}
@@ -90,7 +90,6 @@ def tile_qwen2vlattention_pa_t_kernel(
             nc.sync.dma_start(out=pair[0], in_=pair[1])
 
         halves = [load_x(grp, 2) for grp in range(3)]
-        start(halves[0][0])
         wraw = ttp.tile([P, 4096], BF16, name="tt", align_bytes=64)
         def load_w(w, c0, c1):
             raw = wraw[:, c0:c1].rearrange("p (g c) -> p g c", g=2)
@@ -98,6 +97,7 @@ def tile_qwen2vlattention_pa_t_kernel(
             return wraw[:, c0:c1].rearrange("p (a c) -> p a c", a=4)
 
         wraw_q = load_w(Wq, 0, 2048)
+        start(halves[0][0])
         wraw_k = load_w(Wk, 2048, 3072)
         wraw_v = load_w(Wv, 3072, 4096)
         start(halves[0][1])
@@ -308,18 +308,21 @@ def tile_qwen2vlattention_pa_t_kernel(
             if s > 2:
                 stage_dtr(s - 2)
             if s == 0:
-                brow_f = const.tile([P, P], F32)
-                nc.vector.tensor_copy(out=brow_f[:], in_=brow_bf[:])
-                bt = psm.tile([P, 256], F32, name="m1")
-                nc.tensor.transpose(bt[:, 0:P], brow_f[:], ident[:])
-                nc.vector.tensor_copy(out=bias_col[:], in_=bt[:, 0:4])
                 w_regroup(0, "vector")
-                w_regroup(1, "scalar")
-                stage_q(0)
+                w_regroup(1, "vector")
                 w_regroup(2, "vector")
                 w_regroup(3, "scalar")
-                for h in range(4):
-                    w_quantise(h)
+                w_quantise(0)
+                w_quantise(1)
+                stage_q(0)
+                w_quantise(2)
+                brow_f = const.tile([P, P], F32)
+                nc.vector.tensor_copy(out=brow_f[:], in_=brow_bf[:])
+                w_quantise(3)
+            if s == 1:
+                bt = psy.tile([P, 512], F32, name="yb")
+                nc.tensor.transpose(bt[:, 0:P], brow_f[:], ident[:])
+                nc.vector.tensor_copy(out=bias_col[:], in_=bt[:, 0:4])
             combines(s, True)
             if s >= 2:
                 r = s - 2
@@ -340,6 +343,9 @@ def tile_qwen2vlattention_pa_t_kernel(
             if 1 <= s <= NROUND:
                 stage_b(s - 1)
                 stage_bv(s - 1)
+            if s == 1:
+                nc.tensor.transpose(bt[:, P : 2 * P], bias_col[:, 3:4].to_broadcast([P, P]), ident[:])
+                nc.vector.tensor_copy(out=bvb[:], in_=bt[:, P : 2 * P])
             combines(s, False)
             if s == 3:
                 load_table(6)

@@ -17,14 +17,15 @@ TS = 16
 M = 1024
 NROUND = 16
 NGROUP = 8
+LAST = NROUND - 1
 XBUFS = 6
 OBUFS = 3
 
 FLOPS = 2 * 4096 * 1024 * 512
 BYTES = 4096 * 1024 * 2 + 1024 * 512 * 2 + 2 * 4096 * 128 * 2 + 512 * 2 + 4096 * 512 * 4
 
-TABLE_BATCHES = ((0, 0, 2), (0, 2, 2), (0, 4, 4), (0, 8, 4), (0, 12, 4), (1, 0, 4), (1, 4, 4), (1, 8, 4), (1, 12, 4))
 TABLE_LOADS = ((0, 0, 2), (0, 2, 2), (0, 4, 4), (0, 8, 4), (0, 12, 4), (1, 0, 8), (1, 8, 8))
+TABLE_BATCHES = ((0, 0, 2, 1), (0, 2, 2, 2), (0, 4, 4, 3), (0, 8, 4, 5), (0, 12, 4, 7), (1, 0, 4, 9), (1, 4, 4, 11), (1, 8, 4, 13), (1, 12, 4, 14))
 
 
 def tile_qwen2vlattention_pa_t_kernel(
@@ -37,6 +38,7 @@ def tile_qwen2vlattention_pa_t_kernel(
         xpool = ctx.enter_context(tc.tile_pool(name="xpool", bufs=XBUFS))
         xgp = ctx.enter_context(tc.tile_pool(name="xgp", bufs=3))
         xcp = ctx.enter_context(tc.tile_pool(name="xcp", bufs=4))
+        xpp = ctx.enter_context(tc.tile_pool(name="xpp", bufs=3))
         ytp = ctx.enter_context(tc.tile_pool(name="ytp", bufs=3))
         ttp = ctx.enter_context(tc.tile_pool(name="ttp", bufs=2))
         outp = ctx.enter_context(tc.tile_pool(name="outp", bufs=OBUFS))
@@ -58,9 +60,6 @@ def tile_qwen2vlattention_pa_t_kernel(
         nc.vector.memset(brow_bf[:], 0.0)
         warm = const.tile([P, 2], F32)
         nc.vector.memset(warm[:], 0.0)
-        nc.scalar.dma_start(out=brow_bf[0:2, :], in_=bq)
-        nc.scalar.dma_start(out=brow_bf[2:3, :], in_=bk)
-        nc.scalar.dma_start(out=brow_bf[3:4, :], in_=bv)
         bvb = const.tile([P, P], F32)
         nc.scalar.activation(out=warm[:, 1:2], in_=warm[:, 0:1], func=ACT.Identity, bias=0.0, scale=1.0)
 
@@ -89,28 +88,36 @@ def tile_qwen2vlattention_pa_t_kernel(
         def start(pair):
             nc.sync.dma_start(out=pair[0], in_=pair[1])
 
-        halves = [load_x(grp, 2) for grp in range(3)]
         wraw = ttp.tile([P, 4096], BF16, name="tt", align_bytes=64)
+
         def load_w(w, c0, c1):
             raw = wraw[:, c0:c1].rearrange("p (g c) -> p g c", g=2)
             nc.sync.dma_start(out=raw, in_=w.rearrange("(g p f) h d -> p g (f h d)", g=2, f=4))
             return wraw[:, c0:c1].rearrange("p (a c) -> p a c", a=4)
 
+        x0, x1 = load_x(0, 2), load_x(1, 2)
         wraw_q = load_w(Wq, 0, 2048)
-        start(halves[0][0])
+        start(x0[0])
+        nc.sync.dma_start(out=brow_bf[0:2, :], in_=bq)
+        nc.sync.dma_start(out=brow_bf[2:3, :], in_=bk)
+        nc.sync.dma_start(out=brow_bf[3:4, :], in_=bv)
         wraw_k = load_w(Wk, 2048, 3072)
         wraw_v = load_w(Wv, 3072, 4096)
-        start(halves[0][1])
+        start(x0[1])
+        start(x1[0])
         load_table(0)
-        start(halves[1][0])
+        start(x1[1])
         load_table(1)
-        start(halves[1][1])
+        x2 = load_x(2, 2)
+        start(x2[0])
         load_table(2)
-        start(halves[2][0])
-        start(halves[2][1])
-        for grp in (3, 4, 5):
-            load_table(grp)
-            start(load_x(grp, 1)[0])
+        start(x2[1])
+        start(load_x(3, 1)[0])
+        load_table(3)
+        start(load_x(4, 1)[0])
+        load_table(4)
+        start(load_x(5, 1)[0])
+        load_table(5)
 
         wg = ttp.tile([P, 4, 2, P, 4], BF16, name="tt", align_bytes=64)
         wc = const.tile([P, 4, 2, P], U32, align_bytes=64)
@@ -144,22 +151,26 @@ def tile_qwen2vlattention_pa_t_kernel(
 
         cs_of = {}
 
-        def combine(k, on_vector):
-            b, t0, tn = TABLE_BATCHES[k]
+        def combine(b, t0, tn):
             rawc, rawsn, r0 = raws[(b, t0)]
-            cst = const.tile([P, tn, 2, P], BF16, name="cs%d" % k)
+            cst = const.tile([P, tn, 2, P], BF16, name="cs%d_%d" % (b, t0))
             for i in range(tn):
                 cs_of[(b, t0 + i)] = (cst, i)
-            moves = [(0, raw_lo, raw_hi, rawc, comp, raw_lo) for raw_lo, raw_hi, comp in ((0, 32, 0), (32, 80, 1), (80, 128, 2))]
+            moves = [(0, lo, hi, rawc, comp, lo) for lo, hi, comp in ((0, 32, 0), (32, 80, 1), (80, 128, 2))]
             moves += [(1, lo, hi, rawsn, comp, s0) for lo, hi, comp, s0 in ((0, 16, 1, 64), (16, 64, 2, 80), (64, 96, 0, 0), (96, 128, 1, 32))]
             for row, lo, hi, raw, comp, s0 in moves:
-                if on_vector:
-                    nc.vector.tensor_copy(out=cst[:, :, row, lo:hi], in_=raw[:, comp, r0 : r0 + tn, s0 : s0 + hi - lo])
-                else:
-                    nc.scalar.copy(out=cst[:, :, row, lo:hi], in_=raw[:, comp, r0 : r0 + tn, s0 : s0 + hi - lo])
+                nc.scalar.copy(out=cst[:, :, row, lo:hi], in_=raw[:, comp, r0 : r0 + tn, s0 : s0 + hi - lo])
 
-        xg_of, xc_of, yt_of, yb_of, tt_of, o_of = {}, {}, {}, {}, {}, {}
+        xp_of, xg_of, xc_of, yt_of, yb_of, v_of, tt_of, o_of = {}, {}, {}, {}, {}, {}, {}, {}
         bias_col = const.tile([P, 4], F32)
+
+        def stage_p(r):
+            words = xin[r // 2][:, 2 * (r % 2) + 1, :].bitcast(F32)
+            xp = xpp.tile([P, 512], F32)
+            xp_of[r] = xp
+            nc.scalar.copy(
+                out=xp[:].rearrange("p (g u r) -> p g u r", g=2, u=2), in_=words.rearrange("p (g r u) -> p g u r", g=2, u=2)
+            )
 
         def stage_a(r):
             xt_in = xin[r // 2]
@@ -170,7 +181,11 @@ def tile_qwen2vlattention_pa_t_kernel(
                 xt = psx.tile([P, 512], F32)
                 for i in range(4):
                     g, u = i // 2, i % 2
-                    nc.tensor.transpose(xt[:, i * P : (i + 1) * P], words[:, 256 * g + u : 256 * (g + 1) : 2], ident[:])
+                    if j == 1 and r in xp_of:
+                        src = xp_of[r][:, i * P : (i + 1) * P]
+                    else:
+                        src = words[:, 256 * g + u : 256 * (g + 1) : 2]
+                    nc.tensor.transpose(xt[:, i * P : (i + 1) * P], src, ident[:])
                 nc.scalar.copy(
                     out=xg[:].rearrange("p (g r u) -> p g r u", g=2, u=2)[:, :, j * P : (j + 1) * P, :],
                     in_=xt[:].rearrange("p (g u r) -> p g r u", g=2, u=2),
@@ -184,8 +199,12 @@ def tile_qwen2vlattention_pa_t_kernel(
 
         def stage_b(r):
             xc, xs = xc_of[r]
-            m0 = psm.tile([P, 2, 256], F32)
-            m1 = psm.tile([P, 256], F32)
+            if r == LAST:
+                m0 = psx.tile([P, 2, 256], F32, name="xt")
+                m1 = psx.tile([P, 256], F32, name="xt")
+            else:
+                m0 = psm.tile([P, 2, 256], F32)
+                m1 = psm.tile([P, 256], F32)
             yt = ytp.tile([P, 3, 256], F32)
             yt_of[r] = yt
             for h in range(3):
@@ -208,14 +227,21 @@ def tile_qwen2vlattention_pa_t_kernel(
 
         def stage_bv(r):
             xc, xs = xc_of[r]
-            ybs = []
+            ybs, vs = [], []
             for j in range(2):
-                yb = psy.tile([P, 512], F32)
-                ybs.append(yb)
+                if r == LAST:
+                    if j == 0:
+                        vb = psm.tile([P, 256], F32, name="m1")
+                    v = vb[:, j * P : (j + 1) * P]
+                else:
+                    yb = psy.tile([P, 512], F32)
+                    ybs.append(yb)
+                    v = yb[:, 384:512]
+                vs.append(v)
                 for g in range(2):
                     c0 = g * 256 + j * P
                     nc.tensor.matmul_mx(
-                        out=yb[:, 384:512],
+                        out=v,
                         lhsT=xc[:, c0 : c0 + P].bitcast(FP8X4),
                         lhsT_scale=xs[:, c0 : c0 + P],
                         rhs=wc[:, 3, g, :].bitcast(FP8X4),
@@ -223,133 +249,146 @@ def tile_qwen2vlattention_pa_t_kernel(
                         start=(g == 0),
                         stop=(g == 1),
                     )
-            yb_of[r] = ybs
+            yb_of[r], v_of[r] = ybs, vs
 
         def stage_dtr(r):
             yt = yt_of[r]
             for j in range(2):
+                if r == LAST:
+                    yb = psy.tile([P, 512], F32)
+                    yb_of[r].append(yb)
                 for h in range(3):
                     nc.tensor.transpose(
                         yb_of[r][j][:, h * P : (h + 1) * P], yt[:, h, j * P : (j + 1) * P], ident[:]
                     )
 
-        def stage_e(r):
+        def slots(r):
             grp = r // 2
+            return grp, 2 * (r % 2), 4 * (grp % 2) + 2 * (r % 2)
+
+        def stage_v(r, j):
+            grp, t4, t8 = slots(r)
+            nc.vector.tensor_tensor(out=o_of[grp // 2][0][:, t8 + j, :], in0=v_of[r][j], in1=bvb[:], op=ALU.add)
+
+        def stage_m(r, j):
+            grp, t4, t8 = slots(r)
+            cst, ci = cs_of[(grp // 4, 4 * (grp % 4) + t4 + j)]
+            nc.vector.tensor_tensor(
+                out=tt_of[grp][:, t4 + j],
+                in0=yb_of[r][j][:, 0:384].rearrange("p (h d) -> p h d", h=3).unsqueeze(1).to_broadcast([P, 2, 3, P]),
+                in1=cst[:, ci].unsqueeze(2).to_broadcast([P, 2, 3, P]),
+                op=ALU.mult,
+            )
+
+        def stage_e(r):
             if r % 4 == 0:
                 ov = outp.tile([P, 8, P], F32)
                 oq = outp.tile([P, 8, 256], F32)
                 ok = outp.tile([P, 8, P], F32)
-                o_of[grp // 2] = (ov, oq, ok)
+                o_of[r // 4] = (ov, oq, ok)
             if r % 2 == 0:
                 tt = ttp.tile([P, 4, 2, 3, P], F32, align_bytes=64)
-                tt_of[grp] = tt
-            tt = tt_of[grp]
-            ov = o_of[grp // 2][0]
-            b = grp // 4
+                tt_of[r // 2] = tt
             for j in range(2):
-                t4 = 2 * (r % 2) + j
-                cst, ci = cs_of[(b, 4 * (grp % 4) + t4)]
-                yb = yb_of[r][j]
-                nc.vector.tensor_tensor(out=ov[:, 4 * (grp % 2) + t4, :], in0=yb[:, 384:512], in1=bvb[:], op=ALU.add)
-                nc.vector.tensor_tensor(
-                    out=tt[:, t4],
-                    in0=yb[:, 0:384].rearrange("p (h d) -> p h d", h=3).unsqueeze(1).to_broadcast([P, 2, 3, P]),
-                    in1=cst[:, ci].unsqueeze(2).to_broadcast([P, 2, 3, P]),
-                    op=ALU.mult,
-                )
+                stage_v(r, j)
+                stage_m(r, j)
 
-        def add_q(grp, ta, tb, engine):
-            tt = tt_of[grp]
-            so = 4 * (grp % 2)
-            oq4 = o_of[grp // 2][1][:, so : so + 4, :].rearrange("p t (h d) -> p t h d", h=2)
+        def add_q(r, half, engine, ja=0, jb=2):
+            grp, t4, t8 = slots(r)
+            tt = tt_of[grp][:, t4 + ja : t4 + jb]
+            oq4 = o_of[grp // 2][1][:, t8 + ja : t8 + jb, :].rearrange("p t (h d) -> p t h d", h=2)
+            lo, hi = 64 * half, 64 - 64 * half
             engine.tensor_tensor(
-                out=oq4[:, ta:tb, :, 0:64], in0=tt[:, ta:tb, 0, 0:2, 0:64], in1=tt[:, ta:tb, 1, 0:2, 64:128],
-                op=ALU.subtract,
+                out=oq4[:, :, :, lo : lo + 64], in0=tt[:, :, 0, 0:2, lo : lo + 64], in1=tt[:, :, 1, 0:2, hi : hi + 64],
+                op=ALU.add if half else ALU.subtract,
             )
+
+        def add_k(r, half, engine, ja=0, jb=2):
+            grp, t4, t8 = slots(r)
+            tt = tt_of[grp][:, t4 + ja : t4 + jb]
+            ok = o_of[grp // 2][2][:, t8 + ja : t8 + jb, :]
+            lo, hi = 64 * half, 64 - 64 * half
             engine.tensor_tensor(
-                out=oq4[:, ta:tb, :, 64:128], in0=tt[:, ta:tb, 0, 0:2, 64:128], in1=tt[:, ta:tb, 1, 0:2, 0:64],
-                op=ALU.add,
+                out=ok[:, :, lo : lo + 64], in0=tt[:, :, 0, 2, lo : lo + 64], in1=tt[:, :, 1, 2, hi : hi + 64],
+                op=ALU.add if half else ALU.subtract,
             )
 
-        def add_k(grp, ta, tb):
-            tt = tt_of[grp]
-            so = 4 * (grp % 2)
-            ok = o_of[grp // 2][2][:, so : so + 4, :]
-            nc.vector.tensor_tensor(
-                out=ok[:, ta:tb, 0:64], in0=tt[:, ta:tb, 0, 2, 0:64], in1=tt[:, ta:tb, 1, 2, 64:128], op=ALU.subtract
-            )
-            nc.vector.tensor_tensor(
-                out=ok[:, ta:tb, 64:128], in0=tt[:, ta:tb, 0, 2, 64:128], in1=tt[:, ta:tb, 1, 2, 0:64], op=ALU.add
-            )
+        def store(which, ra, rb):
+            pair = ra // 4
+            t0, ta, tb = 8 * (pair % 2), 2 * (ra % 4), 2 * (ra % 4) + 2 * (rb - ra)
+            view = (v_view, q_view, k_view)[which]
+            nc.sync.dma_start(out=view[pair // 2, :, t0 + ta : t0 + tb, :], in_=o_of[pair][which][:, ta:tb, :])
 
-        def stores(pair, ta, tb):
-            b, t0 = pair // 2, 8 * (pair % 2)
-            ov, oq, ok = o_of[pair]
-            nc.sync.dma_start(out=v_view[b, :, t0 + ta : t0 + tb, :], in_=ov[:, ta:tb, :])
-            nc.sync.dma_start(out=q_view[b, :, t0 + ta : t0 + tb, :], in_=oq[:, ta:tb, :])
-            nc.sync.dma_start(out=k_view[b, :, t0 + ta : t0 + tb, :], in_=ok[:, ta:tb, :])
-
-        first_round = [(8 * b + t0 // 2) for b, t0, tn in TABLE_BATCHES]
-        n_batches = len(TABLE_BATCHES)
-
-        def combines(s, on_vector):
-            for k in range(n_batches):
-                if (k < 2) != on_vector:
-                    continue
-                if s == first_round[k] + (2 if k < 2 else 1):
-                    combine(k, on_vector)
-
-        for s in range(NROUND + 2):
-            pending = []
-            if 2 <= s <= 2:
-                stage_dtr(s - 2)
-            if s < NROUND:
-                stage_a(s)
+        for s in range(NROUND):
+            if s == 2:
+                stage_dtr(0)
+            stage_a(s)
+            if 2 <= s < LAST:
+                stage_p(s + 1)
             if s > 2:
                 stage_dtr(s - 2)
             if s == 0:
                 w_regroup(0, "vector")
                 w_regroup(1, "vector")
-                w_regroup(2, "vector")
-                w_regroup(3, "scalar")
-                w_quantise(0)
-                w_quantise(1)
-                stage_q(0)
-                w_quantise(2)
                 brow_f = const.tile([P, P], F32)
                 nc.vector.tensor_copy(out=brow_f[:], in_=brow_bf[:])
-                w_quantise(3)
-            if s == 1:
                 bt = psy.tile([P, 512], F32, name="yb")
                 nc.tensor.transpose(bt[:, 0:P], brow_f[:], ident[:])
+                w_quantise(0)
+                w_regroup(2, "vector")
+                w_regroup(3, "scalar")
+                w_quantise(1)
                 nc.vector.tensor_copy(out=bias_col[:], in_=bt[:, 0:4])
-            combines(s, True)
+                stage_q(0)
+                w_quantise(2)
+                w_quantise(3)
             if s >= 2:
-                r = s - 2
-                stage_e(r)
-                grp = r // 2
-                ta = 2 * (r % 2)
-                add_q(grp, ta, ta + 2, nc.vector if r == NROUND - 1 else nc.gpsimd)
-                if grp == NGROUP - 1:
-                    pending.append((grp // 2, 4 + ta, 4 + ta + 2))
-                elif r % 2 == 1 and grp == NGROUP - 2:
-                    pending.append((grp // 2, 0, 4))
-                elif r % 4 == 3:
-                    pending.append((grp // 2, 0, 8))
-            if 0 < s < NROUND:
+                stage_e(s - 2)
+                add_q(s - 2, 0, nc.gpsimd)
+                add_q(s - 2, 1, nc.gpsimd)
+                add_k(s - 2, 0, nc.gpsimd)
+            if 0 < s:
                 stage_q(s)
             if s >= 2:
-                add_k((s - 2) // 2, 2 * (s % 2), 2 * (s % 2) + 2)
-            if 1 <= s <= NROUND:
+                add_k(s - 2, 1, nc.vector if s < LAST else nc.gpsimd)
+            if s >= 1:
                 stage_b(s - 1)
                 stage_bv(s - 1)
             if s == 1:
                 nc.tensor.transpose(bt[:, P : 2 * P], bias_col[:, 3:4].to_broadcast([P, P]), ident[:])
                 nc.vector.tensor_copy(out=bvb[:], in_=bt[:, P : 2 * P])
-            combines(s, False)
-            if s == 3:
+            for b, t0, tn, at in TABLE_BATCHES:
+                if at == s:
+                    combine(b, t0, tn)
+            if s in (1, 3):
+                start(load_x(6 + s // 2, 1)[0])
+            if s == 1:
                 load_table(6)
-            if s % 2 == 1 and s // 2 + XBUFS < NGROUP:
-                start(load_x(s // 2 + XBUFS, 1)[0])
-            for pair, ta, tb in pending:
-                stores(pair, ta, tb)
+            r = s - 2
+            if r in (3, 7, 11):
+                for which in range(3):
+                    store(which, r - 3, r + 1)
+        stage_b(LAST)
+        stage_bv(LAST)
+        for which in range(3):
+            store(which, LAST - 3, LAST - 1)
+        r = LAST - 1
+        stage_dtr(r)
+        stage_e(r)
+        for half in range(2):
+            add_q(r, half, nc.gpsimd)
+        for half in range(2):
+            add_k(r, half, nc.gpsimd)
+        for which in range(3):
+            store(which, r, r + 1)
+        r = LAST
+        stage_dtr(r)
+        stage_e(r)
+        store(0, r, r + 1)
+        for half in range(2):
+            add_q(r, half, nc.gpsimd, 0, 1)
+            add_k(r, half, nc.vector)
+        for half in range(2):
+            add_q(r, half, nc.vector, 1, 2)
+        store(2, r, r + 1)
+        store(1, r, r + 1)

@@ -38,7 +38,6 @@ def tile_qwen2vlattention_pa_t_kernel(
         xpool = ctx.enter_context(tc.tile_pool(name="xpool", bufs=XBUFS))
         xgp = ctx.enter_context(tc.tile_pool(name="xgp", bufs=3))
         xcp = ctx.enter_context(tc.tile_pool(name="xcp", bufs=4))
-        xpp = ctx.enter_context(tc.tile_pool(name="xpp", bufs=3))
         ytp = ctx.enter_context(tc.tile_pool(name="ytp", bufs=3))
         ttp = ctx.enter_context(tc.tile_pool(name="ttp", bufs=2))
         outp = ctx.enter_context(tc.tile_pool(name="outp", bufs=OBUFS))
@@ -156,21 +155,17 @@ def tile_qwen2vlattention_pa_t_kernel(
             cst = const.tile([P, tn, 2, P], BF16, name="cs%d_%d" % (b, t0))
             for i in range(tn):
                 cs_of[(b, t0 + i)] = (cst, i)
-            moves = [(0, lo, hi, rawc, comp, lo) for lo, hi, comp in ((0, 32, 0), (32, 80, 1), (80, 128, 2))]
-            moves += [(1, lo, hi, rawsn, comp, s0) for lo, hi, comp, s0 in ((0, 16, 1, 64), (16, 64, 2, 80), (64, 96, 0, 0), (96, 128, 1, 32))]
-            for row, lo, hi, raw, comp, s0 in moves:
-                nc.scalar.copy(out=cst[:, :, row, lo:hi], in_=raw[:, comp, r0 : r0 + tn, s0 : s0 + hi - lo])
+            for lo, hi, comp in ((0, 32, 0), (32, 80, 1), (80, 128, 2)):
+                nc.scalar.copy(out=cst[:, :, 0, lo:hi], in_=rawc[:, comp, r0 : r0 + tn, lo:hi])
+            for lo, hi, comp in ((0, 32, 0), (32, 64, 1)):
+                nc.scalar.activation(
+                    out=cst[:, :, 1, lo:hi], in_=rawsn[:, comp, r0 : r0 + tn, lo:hi], func=ACT.Identity, bias=0.0, scale=-1.0
+                )
+            for lo, hi, comp in ((64, 80, 1), (80, 128, 2)):
+                nc.scalar.copy(out=cst[:, :, 1, lo:hi], in_=rawsn[:, comp, r0 : r0 + tn, lo:hi])
 
-        xp_of, xg_of, xc_of, yt_of, yb_of, v_of, tt_of, o_of = {}, {}, {}, {}, {}, {}, {}, {}
+        xg_of, xc_of, yt_of, yb_of, v_of, tt_of, o_of = {}, {}, {}, {}, {}, {}, {}
         bias_col = const.tile([P, 4], F32)
-
-        def stage_p(r):
-            words = xin[r // 2][:, 2 * (r % 2) + 1, :].bitcast(F32)
-            xp = xpp.tile([P, 512], F32)
-            xp_of[r] = xp
-            nc.scalar.copy(
-                out=xp[:].rearrange("p (g u r) -> p g u r", g=2, u=2), in_=words.rearrange("p (g r u) -> p g u r", g=2, u=2)
-            )
 
         def stage_a(r):
             xt_in = xin[r // 2]
@@ -181,11 +176,7 @@ def tile_qwen2vlattention_pa_t_kernel(
                 xt = psx.tile([P, 512], F32)
                 for i in range(4):
                     g, u = i // 2, i % 2
-                    if j == 1 and r in xp_of:
-                        src = xp_of[r][:, i * P : (i + 1) * P]
-                    else:
-                        src = words[:, 256 * g + u : 256 * (g + 1) : 2]
-                    nc.tensor.transpose(xt[:, i * P : (i + 1) * P], src, ident[:])
+                    nc.tensor.transpose(xt[:, i * P : (i + 1) * P], words[:, 256 * g + u : 256 * (g + 1) : 2], ident[:])
                 nc.scalar.copy(
                     out=xg[:].rearrange("p (g r u) -> p g r u", g=2, u=2)[:, :, j * P : (j + 1) * P, :],
                     in_=xt[:].rearrange("p (g u r) -> p g r u", g=2, u=2),
@@ -200,15 +191,16 @@ def tile_qwen2vlattention_pa_t_kernel(
         def stage_b(r):
             xc, xs = xc_of[r]
             if r == LAST:
-                m0 = psx.tile([P, 2, 256], F32, name="xt")
-                m1 = psx.tile([P, 256], F32, name="xt")
+                m0 = psx.tile([P, 512], F32, name="xt")
+                m1 = psx.tile([P, 512], F32, name="xt")
             else:
-                m0 = psm.tile([P, 2, 256], F32)
-                m1 = psm.tile([P, 256], F32)
+                m0 = psm.tile([P, 512], F32)
+                m1 = psm.tile([P, 512], F32)
             yt = ytp.tile([P, 3, 256], F32)
             yt_of[r] = yt
-            for h in range(3):
-                acc = m0[:, h, :] if h < 2 else m1[:]
+            v_of[r] = m1[:, 256:512].rearrange("p (j d) -> p j d", j=2)
+
+            def head(h, acc):
                 for g in range(2):
                     nc.tensor.matmul_mx(
                         out=acc,
@@ -219,29 +211,15 @@ def tile_qwen2vlattention_pa_t_kernel(
                         start=(g == 0),
                         stop=(g == 1),
                     )
-            for h in range(3):
-                acc = m0[:, h, :] if h < 2 else m1[:]
-                nc.scalar.activation(
-                    out=yt[:, h, :], in_=acc, func=ACT.Identity, bias=bias_col[:, h : h + 1], scale=1.0
-                )
 
-        def stage_bv(r):
-            xc, xs = xc_of[r]
-            ybs, vs = [], []
+            accs = (m0[:, 0:256], m0[:, 256:512], m1[:, 0:256])
+            head(0, accs[0])
+            head(1, accs[1])
             for j in range(2):
-                if r == LAST:
-                    if j == 0:
-                        vb = psm.tile([P, 256], F32, name="m1")
-                    v = vb[:, j * P : (j + 1) * P]
-                else:
-                    yb = psy.tile([P, 512], F32)
-                    ybs.append(yb)
-                    v = yb[:, 384:512]
-                vs.append(v)
                 for g in range(2):
                     c0 = g * 256 + j * P
                     nc.tensor.matmul_mx(
-                        out=v,
+                        out=m1[:, 256 + j * P : 256 + (j + 1) * P],
                         lhsT=xc[:, c0 : c0 + P].bitcast(FP8X4),
                         lhsT_scale=xs[:, c0 : c0 + P],
                         rhs=wc[:, 3, g, :].bitcast(FP8X4),
@@ -249,35 +227,57 @@ def tile_qwen2vlattention_pa_t_kernel(
                         start=(g == 0),
                         stop=(g == 1),
                     )
-            yb_of[r], v_of[r] = ybs, vs
+            head(2, accs[2])
+            for h in range(3):
+                nc.scalar.activation(
+                    out=yt[:, h, :], in_=accs[h], func=ACT.Identity, bias=bias_col[:, h : h + 1], scale=1.0
+                )
 
         def stage_dtr(r):
             yt = yt_of[r]
+            yb_of[r] = []
             for j in range(2):
-                if r == LAST:
-                    yb = psy.tile([P, 512], F32)
-                    yb_of[r].append(yb)
+                yb = psy.tile([P, 384], F32)
+                yb_of[r].append(yb)
                 for h in range(3):
-                    nc.tensor.transpose(
-                        yb_of[r][j][:, h * P : (h + 1) * P], yt[:, h, j * P : (j + 1) * P], ident[:]
-                    )
+                    nc.tensor.transpose(yb[:, h * P : (h + 1) * P], yt[:, h, j * P : (j + 1) * P], ident[:])
 
         def slots(r):
             grp = r // 2
             return grp, 2 * (r % 2), 4 * (grp % 2) + 2 * (r % 2)
 
-        def stage_v(r, j):
+        def stage_v(r):
             grp, t4, t8 = slots(r)
-            nc.vector.tensor_tensor(out=o_of[grp // 2][0][:, t8 + j, :], in0=v_of[r][j], in1=bvb[:], op=ALU.add)
+            nc.vector.tensor_tensor(
+                out=o_of[grp // 2][0][:, t8 : t8 + 2, :], in0=v_of[r],
+                in1=bvb[:].unsqueeze(1).to_broadcast([P, 2, P]), op=ALU.add,
+            )
 
-        def stage_m(r, j):
+        def stage_m(r, j, row):
             grp, t4, t8 = slots(r)
             cst, ci = cs_of[(grp // 4, 4 * (grp % 4) + t4 + j)]
+            y = yb_of[r][j][:].rearrange("p (h a d) -> p h a d", h=3, a=2)
+            if row == 1:
+                y = y[:, :, ::-1, :]
             nc.vector.tensor_tensor(
-                out=tt_of[grp][:, t4 + j],
-                in0=yb_of[r][j][:, 0:384].rearrange("p (h d) -> p h d", h=3).unsqueeze(1).to_broadcast([P, 2, 3, P]),
-                in1=cst[:, ci].unsqueeze(2).to_broadcast([P, 2, 3, P]),
+                out=tt_of[grp][:, t4 + j, row].rearrange("p h (a d) -> p h a d", a=2),
+                in0=y,
+                in1=cst[:, ci, row].rearrange("p (a d) -> p a d", a=2).unsqueeze(1).to_broadcast([P, 3, 2, 64]),
                 op=ALU.mult,
+            )
+
+        def add_q(r, engine, ja=0, jb=2):
+            grp, t4, t8 = slots(r)
+            tt = tt_of[grp][:, t4 + ja : t4 + jb, :, 0:2, :].rearrange("p t r h d -> p t r (h d)")
+            engine.tensor_tensor(
+                out=o_of[grp // 2][1][:, t8 + ja : t8 + jb, :], in0=tt[:, :, 0, :], in1=tt[:, :, 1, :], op=ALU.add
+            )
+
+        def add_k(r):
+            grp, t4, t8 = slots(r)
+            tt = tt_of[grp][:, t4 : t4 + 2]
+            nc.vector.tensor_tensor(
+                out=o_of[grp // 2][2][:, t8 : t8 + 2, :], in0=tt[:, :, 0, 2, :], in1=tt[:, :, 1, 2, :], op=ALU.add
             )
 
         def stage_e(r):
@@ -289,29 +289,13 @@ def tile_qwen2vlattention_pa_t_kernel(
             if r % 2 == 0:
                 tt = ttp.tile([P, 4, 2, 3, P], F32, align_bytes=64)
                 tt_of[r // 2] = tt
-            for j in range(2):
-                stage_v(r, j)
-                stage_m(r, j)
-
-        def add_q(r, half, engine, ja=0, jb=2):
-            grp, t4, t8 = slots(r)
-            tt = tt_of[grp][:, t4 + ja : t4 + jb]
-            oq4 = o_of[grp // 2][1][:, t8 + ja : t8 + jb, :].rearrange("p t (h d) -> p t h d", h=2)
-            lo, hi = 64 * half, 64 - 64 * half
-            engine.tensor_tensor(
-                out=oq4[:, :, :, lo : lo + 64], in0=tt[:, :, 0, 0:2, lo : lo + 64], in1=tt[:, :, 1, 0:2, hi : hi + 64],
-                op=ALU.add if half else ALU.subtract,
-            )
-
-        def add_k(r, half, engine, ja=0, jb=2):
-            grp, t4, t8 = slots(r)
-            tt = tt_of[grp][:, t4 + ja : t4 + jb]
-            ok = o_of[grp // 2][2][:, t8 + ja : t8 + jb, :]
-            lo, hi = 64 * half, 64 - 64 * half
-            engine.tensor_tensor(
-                out=ok[:, :, lo : lo + 64], in0=tt[:, :, 0, 2, lo : lo + 64], in1=tt[:, :, 1, 2, hi : hi + 64],
-                op=ALU.add if half else ALU.subtract,
-            )
+            stage_v(r)
+            stage_m(r, 0, 0)
+            stage_m(r, 0, 1)
+            stage_m(r, 1, 0)
+            if r > 0:
+                add_k(r - 1)
+            stage_m(r, 1, 1)
 
         def store(which, ra, rb):
             pair = ra // 4
@@ -323,8 +307,6 @@ def tile_qwen2vlattention_pa_t_kernel(
             if s == 2:
                 stage_dtr(0)
             stage_a(s)
-            if 2 <= s < LAST:
-                stage_p(s + 1)
             if s > 2:
                 stage_dtr(s - 2)
             if s == 0:
@@ -344,16 +326,11 @@ def tile_qwen2vlattention_pa_t_kernel(
                 w_quantise(3)
             if s >= 2:
                 stage_e(s - 2)
-                add_q(s - 2, 0, nc.gpsimd)
-                add_q(s - 2, 1, nc.gpsimd)
-                add_k(s - 2, 0, nc.gpsimd)
+                add_q(s - 2, nc.gpsimd)
             if 0 < s:
                 stage_q(s)
-            if s >= 2:
-                add_k(s - 2, 1, nc.vector if s < LAST else nc.gpsimd)
             if s >= 1:
                 stage_b(s - 1)
-                stage_bv(s - 1)
             if s == 1:
                 nc.tensor.transpose(bt[:, P : 2 * P], bias_col[:, 3:4].to_broadcast([P, P]), ident[:])
                 nc.vector.tensor_copy(out=bvb[:], in_=bt[:, P : 2 * P])
@@ -366,29 +343,27 @@ def tile_qwen2vlattention_pa_t_kernel(
                 load_table(6)
             r = s - 2
             if r in (3, 7, 11):
-                for which in range(3):
-                    store(which, r - 3, r + 1)
-        stage_b(LAST)
-        stage_bv(LAST)
-        for which in range(3):
+                store(0, r - 3, r + 1)
+                store(1, r - 3, r + 1)
+            if r in (4, 8, 12):
+                store(2, r - 4, r)
+        for which in range(2):
             store(which, LAST - 3, LAST - 1)
         r = LAST - 1
         stage_dtr(r)
+        stage_b(LAST)
         stage_e(r)
-        for half in range(2):
-            add_q(r, half, nc.gpsimd)
-        for half in range(2):
-            add_k(r, half, nc.gpsimd)
-        for which in range(3):
-            store(which, r, r + 1)
+        add_q(r, nc.gpsimd)
+        store(2, LAST - 3, LAST - 1)
+        store(0, r, r + 1)
+        store(1, r, r + 1)
         r = LAST
         stage_dtr(r)
         stage_e(r)
+        store(2, r - 1, r)
         store(0, r, r + 1)
-        for half in range(2):
-            add_q(r, half, nc.gpsimd, 0, 1)
-            add_k(r, half, nc.vector)
-        for half in range(2):
-            add_q(r, half, nc.vector, 1, 2)
-        store(2, r, r + 1)
+        add_q(r, nc.vector, 0, 1)
+        add_q(r, nc.vector, 1, 2)
+        add_k(r)
         store(1, r, r + 1)
+        store(2, r, r + 1)

from contextlib import ExitStack

import concourse.mybir as mybir
from concourse.masks import make_identity

F32 = mybir.dt.float32
BF16 = mybir.dt.bfloat16
U32 = mybir.dt.uint32
U8 = mybir.dt.uint8
FP8X4 = mybir.dt.float8_e4m3fn_x4
ALU = mybir.AluOpType
ACT = mybir.ActivationFunctionType

P = 128
NB = 2
TS = 16
M = 1024
NROUND = 16
NGROUP = 8
LAST = NROUND - 1
XBUFS = 6
OBUFS = 3

FLOPS = 2 * 4096 * 1024 * 512
BYTES = 4096 * 1024 * 2 + 1024 * 512 * 2 + 2 * 4096 * 128 * 2 + 512 * 2 + 4096 * 512 * 4

TABLE_LOADS = ((0, 0, 2), (0, 2, 2), (0, 4, 4), (0, 8, 4), (0, 12, 4), (1, 0, 8), (1, 8, 8))
TABLE_BATCHES = ((0, 0, 2, 1), (0, 2, 2, 2), (0, 4, 4, 3), (0, 8, 4, 5), (0, 12, 4, 7), (1, 0, 4, 9), (1, 4, 4, 11), (1, 8, 4, 13), (1, 12, 4, 14))


def tile_qwen2vlattention_pa_t_kernel(
    tc, hidden_states, cos, sin, Wq, bq, Wk, bk, Wv, bv, out_0, out_1, out_2
):
    nc = tc.nc
    with ExitStack() as ctx:
        ctx.enter_context(tc.manual_schedule())
        const = ctx.enter_context(tc.tile_pool(name="const", bufs=1))
        xpool = ctx.enter_context(tc.tile_pool(name="xpool", bufs=XBUFS))
        xgp = ctx.enter_context(tc.tile_pool(name="xgp", bufs=3))
        xcp = ctx.enter_context(tc.tile_pool(name="xcp", bufs=4))
        ytp = ctx.enter_context(tc.tile_pool(name="ytp", bufs=3))
        ttp = ctx.enter_context(tc.tile_pool(name="ttp", bufs=2))
        outp = ctx.enter_context(tc.tile_pool(name="outp", bufs=OBUFS))
        psx = ctx.enter_context(tc.psum_pool(name="psx", bufs=2))
        psm = ctx.enter_context(tc.psum_pool(name="psm", bufs=1))
        psy = ctx.enter_context(tc.psum_pool(name="psy", bufs=4))

        x_view = hidden_states.rearrange("b (p t) m -> b p t m", t=TS)
        cos_view = cos.rearrange("c b (p t) d -> b p c t d", t=TS)
        sin_view = sin.rearrange("c b (p t) d -> b p c t d", t=TS)
        q_view = out_0.rearrange("b (p t) h d -> b p t (h d)", t=TS)
        k_view = out_1.rearrange("b (p t) h d -> b p t (h d)", t=TS)
        v_view = out_2.rearrange("b (p t) h d -> b p t (h d)", t=TS)

        ident = const.tile([P, P], F32)
        make_identity(nc, ident[:])

        brow_bf = const.tile([P, P], BF16)
        nc.vector.memset(brow_bf[:], 0.0)
        warm = const.tile([P, 2], F32)
        nc.vector.memset(warm[:], 0.0)
        bvb = const.tile([P, P], F32)
        nc.scalar.activation(out=warm[:, 1:2], in_=warm[:, 0:1], func=ACT.Identity, bias=0.0, scale=1.0)

        xin = {}
        raws = {}

        def load_x(grp, parts):
            xt_in = xpool.tile([P, 4, M], BF16, name="xin")
            xin[grp] = xt_in
            b, t0 = grp // 4, 4 * (grp % 4)
            step = 4 // parts
            return [
                (xt_in[:, i * step : (i + 1) * step, :], x_view[b, :, t0 + i * step : t0 + (i + 1) * step, :])
                for i in range(parts)
            ]

        def load_table(k):
            b, t0, tn = TABLE_LOADS[k]
            rawc = const.tile([P, 3, tn, P], BF16, name="rawc%d" % k)
            nc.sync.dma_start(out=rawc[:], in_=cos_view[b, :, :, t0 : t0 + tn, :])
            rawsn = const.tile([P, 3, tn, P], BF16, name="rawsn%d" % k)
            nc.sync.dma_start(out=rawsn[:], in_=sin_view[b, :, :, t0 : t0 + tn, :])
            for i in range(tn):
                raws[(b, t0 + i)] = (rawc, rawsn, i)

        def start(pair):
            nc.sync.dma_start(out=pair[0], in_=pair[1])

        wraw = ttp.tile([P, 4096], BF16, name="tt", align_bytes=64)

        def load_w(w, c0, c1):
            raw = wraw[:, c0:c1].rearrange("p (g c) -> p g c", g=2)
            nc.sync.dma_start(out=raw, in_=w.rearrange("(g p f) h d -> p g (f h d)", g=2, f=4))
            return wraw[:, c0:c1].rearrange("p (a c) -> p a c", a=4)

        x0, x1 = load_x(0, 2), load_x(1, 2)
        wraw_q = load_w(Wq, 0, 2048)
        start(x0[0])
        nc.sync.dma_start(out=brow_bf[0:2, :], in_=bq)
        nc.sync.dma_start(out=brow_bf[2:3, :], in_=bk)
        nc.sync.dma_start(out=brow_bf[3:4, :], in_=bv)
        wraw_k = load_w(Wk, 2048, 3072)
        wraw_v = load_w(Wv, 3072, 4096)
        start(x0[1])
        start(x1[0])
        load_table(0)
        start(x1[1])
        load_table(1)
        x2 = load_x(2, 2)
        start(x2[0])
        load_table(2)
        start(x2[1])
        start(load_x(3, 1)[0])
        load_table(3)
        start(load_x(4, 1)[0])
        load_table(4)
        start(load_x(5, 1)[0])
        load_table(5)

        wg = ttp.tile([P, 4, 2, P, 4], BF16, name="tt", align_bytes=64)
        wc = const.tile([P, 4, 2, P], U32, align_bytes=64)
        ws = const.tile([P, 4, 2, P], U8, align_bytes=64)

        def w_source(h):
            if h < 2:
                v5 = wraw_q.rearrange("p (g u) (e c) -> p g u e c", g=2, e=2)
                return v5[:, :, :, :, h * P : (h + 1) * P]
            raw = wraw_k if h == 2 else wraw_v
            return raw.rearrange("p (g u) (e c) -> p g u e c", g=2, e=2)

        def w_regroup(h, engine):
            src5 = w_source(h)
            for g in range(2):
                dst = wg[:, h, g].rearrange("p c (u e) -> p c u e", u=2)
                src = src5[:, g].rearrange("p u e c -> p c u e")
                if engine == "scalar":
                    nc.scalar.copy(out=dst, in_=src)
                elif engine == "gpsimd":
                    nc.gpsimd.tensor_scalar(out=dst, in0=src, scalar1=1.0, scalar2=0.0, op0=ALU.mult, op1=ALU.add)
                else:
                    nc.vector.tensor_copy(out=dst, in_=src)

        def w_quantise(h):
            nc.vector.quantize_mx(
                out=wc[:, h].rearrange("p g c -> p (g c)").bitcast(FP8X4),
                scales=ws[:, h].rearrange("p g c -> p (g c)"),
                in_=wg[:, h].rearrange("p g c t -> p (g c t)"),
            )

        cs_of = {}

        def combine(b, t0, tn):
            rawc, rawsn, r0 = raws[(b, t0)]
            cst = const.tile([P, tn, 2, P], BF16, name="cs%d_%d" % (b, t0))
            for i in range(tn):
                cs_of[(b, t0 + i)] = (cst, i)
            for lo, hi, comp in ((0, 32, 0), (32, 80, 1), (80, 128, 2)):
                nc.scalar.copy(out=cst[:, :, 0, lo:hi], in_=rawc[:, comp, r0 : r0 + tn, lo:hi])
            for lo, hi, comp in ((0, 32, 0), (32, 64, 1)):
                nc.scalar.activation(
                    out=cst[:, :, 1, lo:hi], in_=rawsn[:, comp, r0 : r0 + tn, lo:hi], func=ACT.Identity, bias=0.0, scale=-1.0
                )
            for lo, hi, comp in ((64, 80, 1), (80, 128, 2)):
                nc.scalar.copy(out=cst[:, :, 1, lo:hi], in_=rawsn[:, comp, r0 : r0 + tn, lo:hi])

        xg_of, xc_of, yt_of, yb_of, v_of, tt_of, o_of = {}, {}, {}, {}, {}, {}, {}
        bias_col = const.tile([P, 4], F32)

        def stage_a(r):
            xt_in = xin[r // 2]
            xg = xgp.tile([P, 1024], F32, align_bytes=64)
            xg_of[r] = xg
            for j in range(2):
                words = xt_in[:, 2 * (r % 2) + j, :].bitcast(F32)
                xt = psx.tile([P, 512], F32)
                for i in range(4):
                    g, u = i // 2, i % 2
                    nc.tensor.transpose(xt[:, i * P : (i + 1) * P], words[:, 256 * g + u : 256 * (g + 1) : 2], ident[:])
                nc.scalar.copy(
                    out=xg[:].rearrange("p (g r u) -> p g r u", g=2, u=2)[:, :, j * P : (j + 1) * P, :],
                    in_=xt[:].rearrange("p (g u r) -> p g r u", g=2, u=2),
                )

        def stage_q(r):
            xc = xcp.tile([P, 512], U32, align_bytes=64)
            xs = xcp.tile([P, 512], U8, align_bytes=64)
            xc_of[r] = (xc, xs)
            nc.vector.quantize_mx(out=xc[:].bitcast(FP8X4), scales=xs[:], in_=xg_of[r][:].bitcast(BF16))

        def stage_b(r):
            xc, xs = xc_of[r]
            if r == LAST:
                m0 = psx.tile([P, 512], F32, name="xt")
                m1 = psx.tile([P, 512], F32, name="xt")
            else:
                m0 = psm.tile([P, 512], F32)
                m1 = psm.tile([P, 512], F32)
            yt = ytp.tile([P, 3, 256], F32)
            yt_of[r] = yt
            v_of[r] = m1[:, 256:512].rearrange("p (j d) -> p j d", j=2)

            def head(h, acc):
                for g in range(2):
                    nc.tensor.matmul_mx(
                        out=acc,
                        lhsT=wc[:, h, g, :].bitcast(FP8X4),
                        lhsT_scale=ws[:, h, g, :],
                        rhs=xc[:, g * 256 : (g + 1) * 256].bitcast(FP8X4),
                        rhs_scale=xs[:, g * 256 : (g + 1) * 256],
                        start=(g == 0),
                        stop=(g == 1),
                    )

            accs = (m0[:, 0:256], m0[:, 256:512], m1[:, 0:256])
            head(0, accs[0])
            head(1, accs[1])
            for j in range(2):
                for g in range(2):
                    c0 = g * 256 + j * P
                    nc.tensor.matmul_mx(
                        out=m1[:, 256 + j * P : 256 + (j + 1) * P],
                        lhsT=xc[:, c0 : c0 + P].bitcast(FP8X4),
                        lhsT_scale=xs[:, c0 : c0 + P],
                        rhs=wc[:, 3, g, :].bitcast(FP8X4),
                        rhs_scale=ws[:, 3, g, :],
                        start=(g == 0),
                        stop=(g == 1),
                    )
            head(2, accs[2])
            for h in range(3):
                nc.scalar.activation(
                    out=yt[:, h, :], in_=accs[h], func=ACT.Identity, bias=bias_col[:, h : h + 1], scale=1.0
                )

        def stage_dtr(r):
            yt = yt_of[r]
            yb_of[r] = []
            for j in range(2):
                yb = psy.tile([P, 384], F32)
                yb_of[r].append(yb)
                for h in range(3):
                    nc.tensor.transpose(yb[:, h * P : (h + 1) * P], yt[:, h, j * P : (j + 1) * P], ident[:])

        def slots(r):
            grp = r // 2
            return grp, 2 * (r % 2), 4 * (grp % 2) + 2 * (r % 2)

        def stage_v(r):
            grp, t4, t8 = slots(r)
            nc.vector.tensor_tensor(
                out=o_of[grp // 2][0][:, t8 : t8 + 2, :], in0=v_of[r],
                in1=bvb[:].unsqueeze(1).to_broadcast([P, 2, P]), op=ALU.add,
            )

        def stage_m(r, j, row):
            grp, t4, t8 = slots(r)
            cst, ci = cs_of[(grp // 4, 4 * (grp % 4) + t4 + j)]
            y = yb_of[r][j][:].rearrange("p (h a d) -> p h a d", h=3, a=2)
            if row == 1:
                y = y[:, :, ::-1, :]
            nc.vector.tensor_tensor(
                out=tt_of[grp][:, t4 + j, row].rearrange("p h (a d) -> p h a d", a=2),
                in0=y,
                in1=cst[:, ci, row].rearrange("p (a d) -> p a d", a=2).unsqueeze(1).to_broadcast([P, 3, 2, 64]),
                op=ALU.mult,
            )

        def add_q(r, engine, ja=0, jb=2):
            grp, t4, t8 = slots(r)
            tt = tt_of[grp][:, t4 + ja : t4 + jb, :, 0:2, :].rearrange("p t r h d -> p t r (h d)")
            engine.tensor_tensor(
                out=o_of[grp // 2][1][:, t8 + ja : t8 + jb, :], in0=tt[:, :, 0, :], in1=tt[:, :, 1, :], op=ALU.add
            )

        def add_k(r):
            grp, t4, t8 = slots(r)
            tt = tt_of[grp][:, t4 : t4 + 2]
            nc.vector.tensor_tensor(
                out=o_of[grp // 2][2][:, t8 : t8 + 2, :], in0=tt[:, :, 0, 2, :], in1=tt[:, :, 1, 2, :], op=ALU.add
            )

        def stage_e(r):
            if r % 4 == 0:
                ov = outp.tile([P, 8, P], F32)
                oq = outp.tile([P, 8, 256], F32)
                ok = outp.tile([P, 8, P], F32)
                o_of[r // 4] = (ov, oq, ok)
            if r % 2 == 0:
                tt = ttp.tile([P, 4, 2, 3, P], F32, align_bytes=64)
                tt_of[r // 2] = tt
            stage_v(r)
            stage_m(r, 0, 0)
            stage_m(r, 0, 1)
            stage_m(r, 1, 0)
            if r > 0:
                add_k(r - 1)
            stage_m(r, 1, 1)

        def store(which, ra, rb):
            pair = ra // 4
            t0, ta, tb = 8 * (pair % 2), 2 * (ra % 4), 2 * (ra % 4) + 2 * (rb - ra)
            view = (v_view, q_view, k_view)[which]
            nc.sync.dma_start(out=view[pair // 2, :, t0 + ta : t0 + tb, :], in_=o_of[pair][which][:, ta:tb, :])

        for s in range(NROUND):
            if s == 2:
                stage_dtr(0)
            stage_a(s)
            if s > 2:
                stage_dtr(s - 2)
            if s == 0:
                w_regroup(0, "vector")
                w_regroup(1, "vector")
                brow_f = const.tile([P, P], F32)
                nc.vector.tensor_copy(out=brow_f[:], in_=brow_bf[:])
                bt = psy.tile([P, 512], F32, name="yb")
                nc.tensor.transpose(bt[:, 0:P], brow_f[:], ident[:])
                w_quantise(0)
                w_regroup(2, "vector")
                w_regroup(3, "scalar")
                w_quantise(1)
                nc.vector.tensor_copy(out=bias_col[:], in_=bt[:, 0:4])
                stage_q(0)
                w_quantise(2)
                w_quantise(3)
            if s >= 2:
                stage_e(s - 2)
                add_q(s - 2, nc.gpsimd)
            if 0 < s:
                stage_q(s)
            if s >= 1:
                stage_b(s - 1)
            if s == 1:
                nc.tensor.transpose(bt[:, P : 2 * P], bias_col[:, 3:4].to_broadcast([P, P]), ident[:])
                nc.vector.tensor_copy(out=bvb[:], in_=bt[:, P : 2 * P])
            for b, t0, tn, at in TABLE_BATCHES:
                if at == s:
                    combine(b, t0, tn)
            if s in (1, 3):
                start(load_x(6 + s // 2, 1)[0])
            if s == 1:
                load_table(6)
            r = s - 2
            if r in (3, 7, 11):
                store(0, r - 3, r + 1)
                store(1, r - 3, r + 1)
            if r in (4, 8, 12):
                store(2, r - 4, r)
        for which in range(2):
            store(which, LAST - 3, LAST - 1)
        r = LAST - 1
        stage_dtr(r)
        stage_b(LAST)
        stage_e(r)
        add_q(r, nc.gpsimd)
        store(2, LAST - 3, LAST - 1)
        store(0, r, r + 1)
        store(1, r, r + 1)
        r = LAST
        stage_dtr(r)
        stage_e(r)
        store(2, r - 1, r)
        store(0, r, r + 1)
        add_q(r, nc.vector, 0, 1)
        add_q(r, nc.vector, 1, 2)
        add_k(r)
        store(1, r, r + 1)
        store(2, r, r + 1)
